import numpy as np
import ml_dtypes


def mxq(x, axis, fmt="e4m3"):
    dtype, down = {"e4m3": (ml_dtypes.float8_e4m3fn, 7), "e5m2": (ml_dtypes.float8_e5m2, 14)}[fmt]
    v = np.moveaxis(np.asarray(x, np.float32).astype(ml_dtypes.bfloat16).astype(np.float64), axis, -1)
    blocks = v.reshape(v.shape[:-1] + (-1, 32))
    amax = np.abs(blocks).max(-1, keepdims=True)
    byte = np.maximum(np.where(amax > 0, np.frexp(amax)[1] - 1 + 127, 0) - down, 1)
    scale = np.exp2(byte - 127.0)
    codes = (blocks / scale).astype(np.float32).astype(dtype).astype(np.float64)
    return np.moveaxis((codes * scale).reshape(v.shape), -1, axis)


WIDE = False


def mx_kscale(k):
    if not WIDE:
        return np.ones(k)
    levels = np.array([10, -10, 5, -5, 0])
    a = np.random.permutation(np.resize(levels, k // 512 * 4)).reshape(k // 512, 4)
    idx = np.arange(k)
    return np.exp2(a[idx // 512, idx % 128 // 32])


BF16 = ml_dtypes.bfloat16


def bf(x):
    return np.asarray(x, np.float32).astype(BF16)


def f64(x):
    return np.asarray(x).astype(np.float64)


B, C, P, D = 64, 512, 128, 512
EPS = 1e-5


def layer_norm(v, w, b):
    m = v.mean(-1, keepdims=True)
    var = ((v - m) ** 2).mean(-1, keepdims=True)
    return (v - m) * (1.0 / np.sqrt(var + EPS)) * w + b


def setup_inputs():
    s = mx_kscale(2 * D)
    return {"prev_cell_out": bf(np.random.standard_normal((B, P, D)) * s[D:]),
            "emb_prompt": bf(np.random.standard_normal((P, D)) / np.sqrt(D)),
            "ln_prompt_w": bf((1.0 + 0.1 * np.random.standard_normal(D)) * s[:D]),
            "ln_prompt_b": bf(0.1 * np.random.standard_normal(D) * s[:D]),
            "W_imp": bf(np.random.standard_normal((2 * D, D)) / D / s[:, None]),
            "b_imp": bf(np.random.standard_normal(D) / np.sqrt(D)),
            "emb_column": bf(0.01 * np.random.standard_normal((C, D))),
            "ln_col_w": bf(1.0 + 0.1 * np.random.standard_normal(D)),
            "ln_col_b": bf(0.1 * np.random.standard_normal(D))}


def reference(prev_cell_out, emb_prompt, ln_prompt_w, ln_prompt_b, W_imp, b_imp, emb_column, ln_col_w, ln_col_b):
    p0 = f64(emb_prompt)
    w = f64(W_imp)
    pn = layer_norm(p0, f64(ln_prompt_w), f64(ln_prompt_b))
    from_prompt = mxq(pn, 1, "e4m3") @ mxq(w[:D], 0, "e4m3")
    from_prev = mxq(f64(prev_cell_out), 2, "e4m3") @ mxq(w[D:], 0, "e4m3")
    x_prompt = from_prompt[None] + from_prev + f64(b_imp) + p0[None]
    col_t = layer_norm(f64(emb_column), f64(ln_col_w), f64(ln_col_b)).T
    return mxq(x_prompt, 2, "e4m3") @ mxq(col_t, 0, "e4m3")

@@ -1,0 +1,333 @@
+from contextlib import ExitStack
+
+import concourse.mybir as mybir
+from concourse.masks import make_identity
+
+F32 = mybir.dt.float32
+BF16 = mybir.dt.bfloat16
+U32 = mybir.dt.uint32
+U8 = mybir.dt.uint8
+FP8X4 = mybir.dt.float8_e4m3fn_x4
+AF = mybir.ActivationFunctionType
+ALU = mybir.AluOpType
+
+P = 128
+D = 512
+NB = 64
+NQ = 16
+NG = 8
+EPS = 1e-5
+FLOPS = 2 * 64 * 128 * 512 * 512 * 2 + 2 * 128 * 512 * 512
+
+
+def tile_tromptcell_pa_t_kernel(
+    tc, prev_cell_out, emb_prompt, ln_prompt_w, ln_prompt_b, W_imp, b_imp, emb_column, ln_col_w, ln_col_b, out
+):
+    nc = tc.nc
+    with ExitStack() as ctx:
+        keep = ctx.enter_context(tc.tile_pool(name="keep", bufs=1))
+        prevp = ctx.enter_context(tc.tile_pool(name="prevp", bufs=6))
+        pgp = ctx.enter_context(tc.tile_pool(name="pgp", bufs=3))
+        pcp = ctx.enter_context(tc.tile_pool(name="pcp", bufs=8))
+        xgp = ctx.enter_context(tc.tile_pool(name="xgp", bufs=2))
+        xcp = ctx.enter_context(tc.tile_pool(name="xcp", bufs=5))
+        outp = ctx.enter_context(tc.tile_pool(name="outp", bufs=5))
+        psA = ctx.enter_context(tc.psum_pool(name="psA", bufs=5))
+        psB = ctx.enter_context(tc.psum_pool(name="psB", bufs=3))
+        ctx.enter_context(tc.manual_schedule())
+
+        prev_v = prev_cell_out.flatten_outer_dims().rearrange("(g q j) d -> g q (j d)", q=P, j=8)
+        out_v = out.flatten_outer_dims().rearrange("(g q j) c -> g q j c", q=P, j=8)
+
+        def regroup_views(dst, src, cs):
+            return (
+                dst[:, cs, :].rearrange("p (c i) t -> p c t i", i=4),
+                src[:, :, cs].rearrange("p t (c i) -> p c t i", i=4),
+            )
+
+        def quantise(name, grouped, width):
+            codes = keep.tile([P, width], U32, name=name + "c", align_bytes=64)
+            scales = keep.tile([P, width], U8, name=name + "s", align_bytes=64)
+            nc.vector.quantize_mx(out=codes[:].bitcast(FP8X4), scales=scales[:], in_=grouped[:].rearrange("p c t -> p (c t)"))
+            return codes, scales
+
+        vrows = keep.tile([P, P], BF16, name="vrows")
+        brow = keep.tile([P, D], BF16, name="brow")
+        ones_b = keep.tile([P, P], BF16, name="ones_b")
+        one_f = keep.tile([P, 1], F32, name="one_f")
+        nc.vector.memset(vrows[:], 0.0)
+        nc.vector.memset(brow[:], 0.0)
+        nc.vector.memset(ones_b[:], 1.0)
+        nc.vector.memset(one_f[:], 1.0)
+        for v, vec in enumerate((ln_prompt_w, ln_prompt_b, ln_col_w, ln_col_b)):
+            nc.scalar.dma_start(out=vrows[4 * v : 4 * v + 4, :], in_=vec.rearrange("(t d) -> t d", t=4))
+        nc.scalar.dma_start(out=brow[0:1, :], in_=b_imp.rearrange("(o d) -> o d", o=1))
+
+        p0 = keep.tile([P, D], BF16, name="p0")
+        nc.sync.dma_start(out=p0[:], in_=emb_prompt)
+        colraw = keep.tile([P, 4, D], BF16, name="colraw")
+        nc.sync.dma_start(out=colraw[:], in_=emb_column.rearrange("(i p) d -> p i d", p=P))
+        w1raw = keep.tile([P, 4, D], BF16, name="w1raw")
+        nc.sync.dma_start(out=w1raw[:], in_=W_imp[0:D, :].rearrange("(t p) c -> p t c", p=P))
+        w2raw = keep.tile([P, 4, D], BF16, name="w2raw")
+        nc.sync.dma_start(
+            out=w2raw[:].rearrange("p (u e) c -> p u (e c)", u=2),
+            in_=W_imp[D : 2 * D, :].rearrange("(u w e) c -> w u (e c)", u=2, e=2),
+        )
+        prev_sb = {}
+
+        def load_prev(g, pieces):
+            t = prevp.tile([P, 8 * D], BF16, name="prev%d" % g, tag="prev")
+            prev_sb[g] = t
+            w = 8 * D // pieces
+            for s in range(pieces):
+                nc.sync.dma_start(out=t[:, s * w : (s + 1) * w], in_=prev_v[g][:, s * w : (s + 1) * w])
+
+        load_prev(0, 2)
+        load_prev(1, 2)
+        for g in range(2, 6):
+            load_prev(g, 1)
+
+        ident_f = keep.tile([P, P], F32, name="ident_f")
+        make_identity(nc, ident_f[:])
+        ident_b = keep.tile([P, P], BF16, name="ident_b")
+        make_identity(nc, ident_b[:])
+        warm = keep.tile([P, 1], F32, name="warm")
+        nc.scalar.activation(out=warm[:], in_=one_f[:], func=AF.Sqrt)
+
+        pc, psc, pgt, xg, xc, xsc, osb, s1t = {}, {}, {}, {}, {}, {}, {}, {}
+        wcol = {}
+
+        def do_T(i):
+            g, h = divmod(i, 2)
+            src = prev_sb[g][:].bitcast(F32)
+            pgt[i] = pgp.tile([P, 4 * D], BF16, name="pg%d" % i, tag="pg", align_bytes=64)
+            pg32 = pgt[i][:].bitcast(F32).rearrange("p (b q u) -> p b q u", b=4, u=2)
+            for half in range(2):
+                tp = psA.tile([P, 2, 2, P], F32, name="tp%d_%d" % (i, half), tag="a")
+                for bb in range(2):
+                    j = 4 * h + 2 * half + bb
+                    for u in range(2):
+                        o = 256 * j + P * u
+                        nc.tensor.transpose(tp[:, bb, u, :], src[:, o : o + P], ident_f[:])
+                nc.scalar.copy(out=pg32[:, 2 * half : 2 * half + 2], in_=tp[:].rearrange("p b u q -> p b q u"))
+
+        def do_QP(i):
+            pc[i] = pcp.tile([P, D], U32, name="pc%d" % i, tag="pc", align_bytes=64)
+            psc[i] = pcp.tile([P, D], U8, name="psc%d" % i, tag="psc", align_bytes=64)
+            nc.vector.quantize_mx(out=pc[i][:].bitcast(FP8X4), scales=psc[i][:], in_=pgt[i][:])
+
+        def do_S1(n):
+            i, b = divmod(n, 4)
+            bs = slice(b * P, (b + 1) * P)
+            s1t[n] = psB.tile([P, 4, P], F32, name="s1_%d" % n, tag="b")
+            for t in range(4):
+                ts = slice(t * P, (t + 1) * P)
+                nc.tensor.matmul_mx(
+                    out=s1t[n][:, t, :], lhsT=wcol["w2c"][:, ts].bitcast(FP8X4), lhsT_scale=wcol["w2s"][:, ts],
+                    rhs=pc[i][:, bs].bitcast(FP8X4), rhs_scale=psc[i][:, bs], start=True, stop=True,
+                )
+
+        def do_XE(n):
+            i, b = divmod(n, 4)
+            if b == 0:
+                xg[i] = xgp.tile([P, 4 * D], BF16, name="xg%d" % i, tag="xg", align_bytes=64)
+            nc.vector.tensor_tensor(
+                out=xg[i][:, b * D : (b + 1) * D].rearrange("p (a b t) -> p a b t", a=8, t=4),
+                in0=s1t[n][:].rearrange("p t (a b) -> p a b t", a=8),
+                in1=wcol["const"][:, n % 8].unsqueeze(1).to_broadcast([P, 8, 16, 4]),
+                op=ALU.add,
+            )
+
+        def do_QX(i, part, parts):
+            if part == 0:
+                xc[i] = xcp.tile([P, D], U32, name="xc%d" % i, tag="xc", align_bytes=64)
+                xsc[i] = xcp.tile([P, D], U8, name="xsc%d" % i, tag="xsc", align_bytes=64)
+            w = D // parts
+            cs = slice(part * w, (part + 1) * w)
+            nc.vector.quantize_mx(
+                out=xc[i][:, cs].bitcast(FP8X4), scales=xsc[i][:, cs], in_=xg[i][:, 4 * part * w : 4 * (part + 1) * w]
+            )
+
+        def do_S2(n):
+            i, b = divmod(n, 4)
+            bs = slice(b * P, (b + 1) * P)
+            s2 = psA.tile([P, D], F32, name="s2_%d" % n, tag="a")
+            nc.tensor.matmul_mx(
+                out=s2[:], lhsT=xc[i][:, bs].bitcast(FP8X4), lhsT_scale=xsc[i][:, bs],
+                rhs=wcol["colc"][:].bitcast(FP8X4), rhs_scale=wcol["cols"][:], start=True, stop=True,
+            )
+            if b == 0:
+                osb[i] = outp.tile([P, 4, D], F32, name="osb%d" % i, tag="osb")
+            if i == NQ - 1 and b % 2 == 1:
+                nc.vector.tensor_copy(out=osb[i][:, b, :], in_=s2[:])
+            else:
+                nc.scalar.copy(out=osb[i][:, b, :], in_=s2[:])
+            g, h = divmod(i, 2)
+            if i == NQ - 1 and b % 2 == 1:
+                nc.sync.dma_start(out=out_v[g][:, 4 * h + b - 1 : 4 * h + b + 1, :], in_=osb[i][:, b - 1 : b + 1, :])
+            elif i < NQ - 1 and b == 3:
+                nc.sync.dma_start(out=out_v[g][:, 4 * h : 4 * h + 4, :], in_=osb[i][:])
+
+        vt_ps = psA.tile([P, P], BF16, name="vt_ps", tag="a")
+        nc.tensor.transpose(vt_ps[:], vrows[:], ident_b[:])
+        vT = keep.tile([P, 16], F32, name="vT")
+        nc.scalar.copy(out=vT[:], in_=vt_ps[:, 0:16])
+
+        c0_ps = psA.tile([P, 4, P], F32, name="c0_ps", tag="a")
+        for t in range(4):
+            nc.tensor.matmul(out=c0_ps[:, t, :], lhsT=p0[:, t * P : (t + 1) * P], rhs=ident_b[:], start=True, stop=False)
+            nc.tensor.matmul(out=c0_ps[:, t, :], lhsT=brow[:, t * P : (t + 1) * P], rhs=ones_b[:], start=False, stop=True)
+
+        st0 = keep.tile([P, 6], F32, name="st0")
+        nc.vector.bn_stats(out=st0[:], in_=p0[:])
+        mv0 = keep.tile([P, 2], F32, name="mv0")
+        nc.vector.bn_aggr(out=mv0[:], in_=st0[:])
+        ve0 = keep.tile([P, 1], F32, name="ve0")
+        nc.vector.tensor_scalar(out=ve0[:], in0=mv0[:, 1:2], scalar1=EPS, scalar2=None, op0=ALU.add)
+        sd0 = keep.tile([P, 1], F32, name="sd0")
+        nc.scalar.activation(out=sd0[:], in_=ve0[:], func=AF.Sqrt)
+        c0_sb = keep.tile([P, 8, 16, 4], F32, name="c0_sb")
+        nc.scalar.copy(out=c0_sb[:], in_=c0_ps[:].rearrange("p t (b j) -> p j b t", j=8))
+
+        stc = keep.tile([P, 4, 6], F32, name="stc")
+        mvc = keep.tile([P, 4, 2], F32, name="mvc")
+
+        def col_stats(i):
+            nc.vector.bn_stats(out=stc[:, i, :], in_=colraw[:, i, :])
+            nc.vector.bn_aggr(out=mvc[:, i, :], in_=stc[:, i, :])
+
+        col_stats(0)
+        rs0 = keep.tile([P, 1], F32, name="rs0")
+        nc.vector.reciprocal(out=rs0[:], in_=sd0[:])
+        col_stats(1)
+        z0 = keep.tile([P, D], F32, name="z0")
+        nc.vector.tensor_scalar(
+            out=z0[:], in0=p0[:], scalar1=mv0[:, 0:1], scalar2=rs0[:, 0:1], op0=ALU.subtract, op1=ALU.mult
+        )
+        zt = []
+        for half in range(2):
+            zt.append(psB.tile([P, 2, P], F32, name="zt%d" % half, tag="b"))
+            for tt in range(2):
+                t = 2 * half + tt
+                nc.tensor.transpose(zt[half][:, tt, :], z0[:, t * P : (t + 1) * P], ident_f[:])
+        col_stats(2)
+        col_stats(3)
+
+        w1g = keep.tile([P, D, 4], BF16, name="w1g", align_bytes=64)
+        w2g = keep.tile([P, D, 4], BF16, name="w2g", align_bytes=64)
+        for s in range(2):
+            dst, src = regroup_views(w1g, w1raw, slice(s * 256, (s + 1) * 256))
+            nc.scalar.copy(out=dst, in_=src)
+        for s in range(2):
+            dst, src = regroup_views(w2g, w2raw, slice(s * 256, (s + 1) * 256))
+            nc.gpsimd.tensor_scalar(out=dst, in0=src, scalar1=1.0, scalar2=0.0, op0=ALU.mult, op1=ALU.add)
+
+        pnp = keep.tile([P, 4, P], BF16, name="pnp")
+        for t in range(2):
+            nc.scalar.activation(
+                out=pnp[:, t, :], in_=zt[0][:, t, :], func=AF.Identity, scale=vT[:, t : t + 1], bias=vT[:, 4 + t : 5 + t]
+            )
+        for t in range(2, 4):
+            nc.vector.tensor_scalar(
+                out=pnp[:, t, :], in0=zt[1][:, t - 2, :], scalar1=vT[:, t : t + 1], scalar2=vT[:, 4 + t : 5 + t],
+                op0=ALU.mult, op1=ALU.add,
+            )
+        w1c, w1s = quantise("w1", w1g, D)
+        png = keep.tile([P, P, 4], BF16, name="png", align_bytes=64)
+        nc.vector.tensor_copy(out=png[:], in_=pnp[:].rearrange("p t q -> p q t"))
+        vec_ = keep.tile([P, 4], F32, name="vec_")
+        nc.vector.tensor_scalar(out=vec_[:], in0=mvc[:, :, 1], scalar1=EPS, scalar2=None, op0=ALU.add)
+        nmc = keep.tile([P, 4], F32, name="nmc")
+        nc.vector.tensor_scalar(out=nmc[:], in0=mvc[:, :, 0], scalar1=-1.0, scalar2=None, op0=ALU.mult)
+
+        do_T(0)
+        sdc = keep.tile([P, 4], F32, name="sdc")
+        nc.scalar.activation(out=sdc[:], in_=vec_[:], func=AF.Sqrt)
+        pnc, pns = quantise("pn", png, P)
+        wcol["w2c"], wcol["w2s"] = quantise("w2", w2g, D)
+        rsc = keep.tile([P, 4], F32, name="rsc")
+        nc.vector.reciprocal(out=rsc[:], in_=sdc[:])
+        zc = keep.tile([P, 4, D], F32, name="zc")
+        for i in range(4):
+            nc.gpsimd.tensor_scalar(
+                out=zc[:, i, :], in0=colraw[:, i, :], scalar1=nmc[:, i : i + 1], scalar2=rsc[:, i : i + 1],
+                op0=ALU.add, op1=ALU.mult,
+            )
+        do_T(1)
+        load_prev(6, 1)
+        fp_ps = psB.tile([P, 4, P], F32, name="fp_ps", tag="b")
+        for t in range(4):
+            ts = slice(t * P, (t + 1) * P)
+            nc.tensor.matmul_mx(
+                out=fp_ps[:, t, :], lhsT=w1c[:, ts].bitcast(FP8X4), lhsT_scale=w1s[:, ts],
+                rhs=pnc[:].bitcast(FP8X4), rhs_scale=pns[:], start=True, stop=True,
+            )
+        wcol["const"] = keep.tile([P, 8, 16, 4], F32, name="const")
+        nc.vector.tensor_tensor(
+            out=wcol["const"][:], in0=fp_ps[:].rearrange("p t (b j) -> p j b t", j=8), in1=c0_sb[:], op=ALU.add
+        )
+        do_QP(0)
+        do_T(2)
+        do_QP(1)
+        do_T(3)
+        load_prev(7, 1)
+        do_QP(2)
+        for n in range(3):
+            do_S1(n)
+
+        colp = keep.tile([P, 4, D], BF16, name="colp")
+        colg = keep.tile([P, D, 4], BF16, name="colg", align_bytes=64)
+
+        def col_transposed():
+            for t in range(4):
+                ct = psA.tile([P, D], F32, name="ct%d" % t, tag="a")
+                for i in range(4):
+                    nc.tensor.transpose(ct[:, i * P : (i + 1) * P], zc[:, i, t * P : (t + 1) * P], ident_f[:])
+                nc.scalar.activation(
+                    out=colp[:, t, :], in_=ct[:], func=AF.Identity, scale=vT[:, 8 + t : 9 + t], bias=vT[:, 12 + t : 13 + t]
+                )
+            for s in range(2):
+                dst, src = regroup_views(colg, colp, slice(s * 256, (s + 1) * 256))
+                nc.gpsimd.tensor_scalar(out=dst, in0=src, scalar1=1.0, scalar2=0.0, op0=ALU.mult, op1=ALU.add)
+
+        t_next, q_next, s2_next = 4, 3, 0
+        for k in range(NQ + 1):
+            last = k == NQ - 1
+            if k < NQ:
+                do_XE(4 * k)
+            if 1 <= k:
+                if k == NQ:
+                    do_QX(k - 1, 1, 2)
+                else:
+                    do_QX(k - 1, 0, 1)
+            if k == 2:
+                wcol["colc"], wcol["cols"] = quantise("col", colg, D)
+            n_s2 = 0
+            if k >= 2:
+                n_s2 = min(4 * k - s2_next, 4 if t_next < NQ else 6)
+                if k == NQ:
+                    n_s2 = NB - s2_next
+            q_end = t_next
+            for b in range(4):
+                if 4 * k + 3 + b < NB:
+                    do_S1(4 * k + 3 + b)
+                if k == 0 and b == 0:
+                    col_transposed()
+                c = -(-n_s2 // (4 - b))
+                n_s2 -= c
+                for r in range(c):
+                    do_S2(s2_next)
+                    s2_next += 1
+            for r in range(2 if k == 1 else 1):
+                if t_next < NQ:
+                    do_T(t_next)
+                    t_next += 1
+            if k < NQ:
+                for b in range(1, 4):
+                    do_XE(4 * k + b)
+                    if last and b == 2:
+                        do_QX(k, 0, 2)
+                while q_next < q_end:
+                    do_QP(q_next)
+                    q_next += 1

@@ -212,16 +212,15 @@ def tile_tromptcell_pa_t_kernel(
                 t = 2 * half + tt
                 nc.tensor.transpose(zt[half][:, tt, :], z0[:, t * P : (t + 1) * P], ident_f[:])
         col_stats(2)
-        col_stats(3)
 
         w1g = keep.tile([P, D, 4], BF16, name="w1g", align_bytes=64)
         w2g = keep.tile([P, D, 4], BF16, name="w2g", align_bytes=64)
-        for s in range(2):
-            dst, src = regroup_views(w1g, w1raw, slice(s * 256, (s + 1) * 256))
+        halves = (slice(0, 256), slice(256, 512))
+        for cs in halves:
+            dst, src = regroup_views(w1g, w1raw, cs)
             nc.scalar.copy(out=dst, in_=src)
-        for s in range(2):
-            dst, src = regroup_views(w2g, w2raw, slice(s * 256, (s + 1) * 256))
-            nc.gpsimd.tensor_scalar(out=dst, in0=src, scalar1=1.0, scalar2=0.0, op0=ALU.mult, op1=ALU.add)
+        dst, src = regroup_views(w2g, w2raw, halves[0])
+        nc.vector.tensor_copy(out=dst, in_=src)
 
         pnp = keep.tile([P, 4, P], BF16, name="pnp")
         for t in range(2):
@@ -233,27 +232,16 @@ def tile_tromptcell_pa_t_kernel(
                 out=pnp[:, t, :], in0=zt[1][:, t - 2, :], scalar1=vT[:, t : t + 1], scalar2=vT[:, 4 + t : 5 + t],
                 op0=ALU.mult, op1=ALU.add,
             )
-        w1c, w1s = quantise("w1", w1g, D)
+        dst, src = regroup_views(w2g, w2raw, halves[1])
+        nc.vector.tensor_copy(out=dst, in_=src)
         png = keep.tile([P, P, 4], BF16, name="png", align_bytes=64)
         nc.vector.tensor_copy(out=png[:], in_=pnp[:].rearrange("p t q -> p q t"))
-        vec_ = keep.tile([P, 4], F32, name="vec_")
-        nc.vector.tensor_scalar(out=vec_[:], in0=mvc[:, :, 1], scalar1=EPS, scalar2=None, op0=ALU.add)
-        nmc = keep.tile([P, 4], F32, name="nmc")
-        nc.vector.tensor_scalar(out=nmc[:], in0=mvc[:, :, 0], scalar1=-1.0, scalar2=None, op0=ALU.mult)
-
-        do_T(0)
-        sdc = keep.tile([P, 4], F32, name="sdc")
-        nc.scalar.activation(out=sdc[:], in_=vec_[:], func=AF.Sqrt)
+        w1c, w1s = quantise("w1", w1g, D)
         pnc, pns = quantise("pn", png, P)
         wcol["w2c"], wcol["w2s"] = quantise("w2", w2g, D)
-        rsc = keep.tile([P, 4], F32, name="rsc")
-        nc.vector.reciprocal(out=rsc[:], in_=sdc[:])
-        zc = keep.tile([P, 4, D], F32, name="zc")
-        for i in range(4):
-            nc.gpsimd.tensor_scalar(
-                out=zc[:, i, :], in0=colraw[:, i, :], scalar1=nmc[:, i : i + 1], scalar2=rsc[:, i : i + 1],
-                op0=ALU.add, op1=ALU.mult,
-            )
+        col_stats(3)
+
+        do_T(0)
         do_T(1)
         load_prev(6, 1)
         fp_ps = psB.tile([P, 4, P], F32, name="fp_ps", tag="b")
@@ -267,11 +255,26 @@ def tile_tromptcell_pa_t_kernel(
         nc.vector.tensor_tensor(
             out=wcol["const"][:], in0=fp_ps[:].rearrange("p t (b j) -> p j b t", j=8), in1=c0_sb[:], op=ALU.add
         )
+        vec_ = keep.tile([P, 4], F32, name="vec_")
+        nc.vector.tensor_scalar(out=vec_[:], in0=mvc[:, :, 1], scalar1=EPS, scalar2=None, op0=ALU.add)
+        nmc = keep.tile([P, 4], F32, name="nmc")
+        nc.vector.tensor_scalar(out=nmc[:], in0=mvc[:, :, 0], scalar1=-1.0, scalar2=None, op0=ALU.mult)
         do_QP(0)
         do_T(2)
+        sdc = keep.tile([P, 4], F32, name="sdc")
+        nc.scalar.activation(out=sdc[:], in_=vec_[:], func=AF.Sqrt)
         do_QP(1)
+        rsc = keep.tile([P, 4], F32, name="rsc")
+        nc.vector.reciprocal(out=rsc[:], in_=sdc[:])
+        nmr = keep.tile([P, 4], F32, name="nmr")
+        nc.vector.tensor_tensor(out=nmr[:], in0=nmc[:], in1=rsc[:], op=ALU.mult)
         do_T(3)
         load_prev(7, 1)
+        zc = keep.tile([P, 4, D], F32, name="zc")
+        for i in range(4):
+            nc.scalar.activation(
+                out=zc[:, i, :], in_=colraw[:, i, :], func=AF.Identity, scale=rsc[:, i : i + 1], bias=nmr[:, i : i + 1]
+            )
         do_QP(2)
         for n in range(3):
             do_S1(n)
@@ -287,9 +290,6 @@ def tile_tromptcell_pa_t_kernel(
                 nc.scalar.activation(
                     out=colp[:, t, :], in_=ct[:], func=AF.Identity, scale=vT[:, 8 + t : 9 + t], bias=vT[:, 12 + t : 13 + t]
                 )
-            for s in range(2):
-                dst, src = regroup_views(colg, colp, slice(s * 256, (s + 1) * 256))
-                nc.gpsimd.tensor_scalar(out=dst, in0=src, scalar1=1.0, scalar2=0.0, op0=ALU.mult, op1=ALU.add)
 
         t_next, q_next, s2_next = 4, 3, 0
         for k in range(NQ + 1):
@@ -312,7 +312,7 @@ def tile_tromptcell_pa_t_kernel(
             for b in range(4):
                 if 4 * k + 3 + b < NB:
                     do_S1(4 * k + 3 + b)
-                if k == 0 and b == 0:
+                if k == 1 and b == 0:
                     col_transposed()
                 c = -(-n_s2 // (4 - b))
                 n_s2 -= c
@@ -331,3 +331,7 @@ def tile_tromptcell_pa_t_kernel(
                 while q_next < q_end:
                     do_QP(q_next)
                     q_next += 1
+            if k == 1:
+                for cs in halves:
+                    dst, src = regroup_views(colg, colp, cs)
+                    nc.vector.tensor_copy(out=dst, in_=src)

@@ -31,7 +31,7 @@ def tile_tromptcell_pa_t_kernel(
         pcp = ctx.enter_context(tc.tile_pool(name="pcp", bufs=8))
         xgp = ctx.enter_context(tc.tile_pool(name="xgp", bufs=2))
         xcp = ctx.enter_context(tc.tile_pool(name="xcp", bufs=5))
-        outp = ctx.enter_context(tc.tile_pool(name="outp", bufs=5))
+        outp = ctx.enter_context(tc.tile_pool(name="outp", bufs=10))
         psA = ctx.enter_context(tc.psum_pool(name="psA", bufs=5))
         psB = ctx.enter_context(tc.psum_pool(name="psB", bufs=3))
         ctx.enter_context(tc.manual_schedule())
@@ -139,15 +139,12 @@ def tile_tromptcell_pa_t_kernel(
                 op=ALU.add,
             )
 
-        def do_QX(i, part, parts):
-            if part == 0:
+        def do_QX(i, b0, b1):
+            if b0 == 0:
                 xc[i] = xcp.tile([P, D], U32, name="xc%d" % i, tag="xc", align_bytes=64)
                 xsc[i] = xcp.tile([P, D], U8, name="xsc%d" % i, tag="xsc", align_bytes=64)
-            w = D // parts
-            cs = slice(part * w, (part + 1) * w)
-            nc.vector.quantize_mx(
-                out=xc[i][:, cs].bitcast(FP8X4), scales=xsc[i][:, cs], in_=xg[i][:, 4 * part * w : 4 * (part + 1) * w]
-            )
+            cs = slice(b0 * P, b1 * P)
+            nc.vector.quantize_mx(out=xc[i][:, cs].bitcast(FP8X4), scales=xsc[i][:, cs], in_=xg[i][:, b0 * D : b1 * D])
 
         def do_S2(n):
             i, b = divmod(n, 4)
@@ -157,17 +154,18 @@ def tile_tromptcell_pa_t_kernel(
                 out=s2[:], lhsT=xc[i][:, bs].bitcast(FP8X4), lhsT_scale=xsc[i][:, bs],
                 rhs=wcol["colc"][:].bitcast(FP8X4), rhs_scale=wcol["cols"][:], start=True, stop=True,
             )
-            if b == 0:
-                osb[i] = outp.tile([P, 4, D], F32, name="osb%d" % i, tag="osb")
-            if i == NQ - 1 and b % 2 == 1:
-                nc.vector.tensor_copy(out=osb[i][:, b, :], in_=s2[:])
+            m, e = divmod(n, 2)
+            if e == 0:
+                osb[m] = outp.tile([P, 2, D], F32, name="osb%d" % m, tag="osb")
+            if i == NQ - 1 and e == 1:
+                nc.vector.tensor_copy(out=osb[m][:, e, :], in_=s2[:])
             else:
-                nc.scalar.copy(out=osb[i][:, b, :], in_=s2[:])
-            g, h = divmod(i, 2)
-            if i == NQ - 1 and b % 2 == 1:
-                nc.sync.dma_start(out=out_v[g][:, 4 * h + b - 1 : 4 * h + b + 1, :], in_=osb[i][:, b - 1 : b + 1, :])
-            elif i < NQ - 1 and b == 3:
-                nc.sync.dma_start(out=out_v[g][:, 4 * h : 4 * h + 4, :], in_=osb[i][:])
+                nc.scalar.copy(out=osb[m][:, e, :], in_=s2[:])
+            g, j = divmod(n, 8)
+            if n >= NB - 2:
+                nc.sync.dma_start(out=out_v[g][:, j, :], in_=osb[m][:, e, :])
+            elif e == 1:
+                nc.sync.dma_start(out=out_v[g][:, j - 1 : j + 1, :], in_=osb[m][:])
 
         vt_ps = psA.tile([P, P], BF16, name="vt_ps", tag="a")
         nc.tensor.transpose(vt_ps[:], vrows[:], ident_b[:])
@@ -296,11 +294,11 @@ def tile_tromptcell_pa_t_kernel(
             last = k == NQ - 1
             if k < NQ:
                 do_XE(4 * k)
-            if 1 <= k:
-                if k == NQ:
-                    do_QX(k - 1, 1, 2)
-                else:
-                    do_QX(k - 1, 0, 1)
+            if 1 <= k < NQ:
+                do_QX(k - 1, 0, 4)
+            if k == NQ:
+                do_QX(k - 1, 2, 3)
+                do_QX(k - 1, 3, 4)
             if k == 2:
                 wcol["colc"], wcol["cols"] = quantise("col", colg, D)
             n_s2 = 0

@@ -32,8 +32,8 @@ def tile_tromptcell_pa_t_kernel(
         xgp = ctx.enter_context(tc.tile_pool(name="xgp", bufs=2))
         xcp = ctx.enter_context(tc.tile_pool(name="xcp", bufs=5))
         outp = ctx.enter_context(tc.tile_pool(name="outp", bufs=10))
-        psA = ctx.enter_context(tc.psum_pool(name="psA", bufs=5))
-        psB = ctx.enter_context(tc.psum_pool(name="psB", bufs=3))
+        psA = ctx.enter_context(tc.psum_pool(name="psA", bufs=4))
+        psB = ctx.enter_context(tc.psum_pool(name="psB", bufs=4))
         ctx.enter_context(tc.manual_schedule())
 
         prev_v = prev_cell_out.flatten_outer_dims().rearrange("(g q j) d -> g q (j d)", q=P, j=8)

@@ -186,19 +186,21 @@ def tile_tromptcell_pa_t_kernel(
         sd0 = keep.tile([P, 1], F32, name="sd0")
         nc.scalar.activation(out=sd0[:], in_=ve0[:], func=AF.Sqrt)
         c0_sb = keep.tile([P, 8, 16, 4], F32, name="c0_sb")
-        nc.scalar.copy(out=c0_sb[:], in_=c0_ps[:].rearrange("p t (b j) -> p j b t", j=8))
 
         stc = keep.tile([P, 4, 6], F32, name="stc")
         mvc = keep.tile([P, 4, 2], F32, name="mvc")
 
         def col_stats(i):
             nc.vector.bn_stats(out=stc[:, i, :], in_=colraw[:, i, :])
+
+        def col_aggr(i):
             nc.vector.bn_aggr(out=mvc[:, i, :], in_=stc[:, i, :])
 
         col_stats(0)
         rs0 = keep.tile([P, 1], F32, name="rs0")
         nc.vector.reciprocal(out=rs0[:], in_=sd0[:])
         col_stats(1)
+        col_aggr(0)
         z0 = keep.tile([P, D], F32, name="z0")
         nc.vector.tensor_scalar(
             out=z0[:], in0=p0[:], scalar1=mv0[:, 0:1], scalar2=rs0[:, 0:1], op0=ALU.subtract, op1=ALU.mult
@@ -210,6 +212,7 @@ def tile_tromptcell_pa_t_kernel(
                 t = 2 * half + tt
                 nc.tensor.transpose(zt[half][:, tt, :], z0[:, t * P : (t + 1) * P], ident_f[:])
         col_stats(2)
+        col_aggr(1)
 
         w1g = keep.tile([P, D, 4], BF16, name="w1g", align_bytes=64)
         w2g = keep.tile([P, D, 4], BF16, name="w2g", align_bytes=64)
@@ -219,12 +222,14 @@ def tile_tromptcell_pa_t_kernel(
             nc.scalar.copy(out=dst, in_=src)
         dst, src = regroup_views(w2g, w2raw, halves[0])
         nc.vector.tensor_copy(out=dst, in_=src)
+        col_aggr(2)
 
         pnp = keep.tile([P, 4, P], BF16, name="pnp")
         for t in range(2):
             nc.scalar.activation(
                 out=pnp[:, t, :], in_=zt[0][:, t, :], func=AF.Identity, scale=vT[:, t : t + 1], bias=vT[:, 4 + t : 5 + t]
             )
+        nc.scalar.copy(out=c0_sb[:], in_=c0_ps[:].rearrange("p t (b j) -> p j b t", j=8))
         for t in range(2, 4):
             nc.vector.tensor_scalar(
                 out=pnp[:, t, :], in0=zt[1][:, t - 2, :], scalar1=vT[:, t : t + 1], scalar2=vT[:, 4 + t : 5 + t],
@@ -236,8 +241,8 @@ def tile_tromptcell_pa_t_kernel(
         nc.vector.tensor_copy(out=png[:], in_=pnp[:].rearrange("p t q -> p q t"))
         w1c, w1s = quantise("w1", w1g, D)
         pnc, pns = quantise("pn", png, P)
-        wcol["w2c"], wcol["w2s"] = quantise("w2", w2g, D)
         col_stats(3)
+        wcol["w2c"], wcol["w2s"] = quantise("w2", w2g, D)
 
         do_T(0)
         do_T(1)
@@ -253,6 +258,7 @@ def tile_tromptcell_pa_t_kernel(
         nc.vector.tensor_tensor(
             out=wcol["const"][:], in0=fp_ps[:].rearrange("p t (b j) -> p j b t", j=8), in1=c0_sb[:], op=ALU.add
         )
+        col_aggr(3)
         vec_ = keep.tile([P, 4], F32, name="vec_")
         nc.vector.tensor_scalar(out=vec_[:], in0=mvc[:, :, 1], scalar1=EPS, scalar2=None, op0=ALU.add)
         nmc = keep.tile([P, 4], F32, name="nmc")
@@ -264,16 +270,16 @@ def tile_tromptcell_pa_t_kernel(
         do_QP(1)
         rsc = keep.tile([P, 4], F32, name="rsc")
         nc.vector.reciprocal(out=rsc[:], in_=sdc[:])
-        nmr = keep.tile([P, 4], F32, name="nmr")
-        nc.vector.tensor_tensor(out=nmr[:], in0=nmc[:], in1=rsc[:], op=ALU.mult)
         do_T(3)
         load_prev(7, 1)
         zc = keep.tile([P, 4, D], F32, name="zc")
+        do_QP(2)
+        nmr = keep.tile([P, 4], F32, name="nmr")
+        nc.vector.tensor_tensor(out=nmr[:], in0=nmc[:], in1=rsc[:], op=ALU.mult)
         for i in range(4):
             nc.scalar.activation(
                 out=zc[:, i, :], in_=colraw[:, i, :], func=AF.Identity, scale=rsc[:, i : i + 1], bias=nmr[:, i : i + 1]
             )
-        do_QP(2)
         for n in range(3):
             do_S1(n)
 
@@ -294,6 +300,10 @@ def tile_tromptcell_pa_t_kernel(
             last = k == NQ - 1
             if k < NQ:
                 do_XE(4 * k)
+            if k == 2:
+                for cs in halves:
+                    dst, src = regroup_views(colg, colp, cs)
+                    nc.vector.tensor_copy(out=dst, in_=src)
             if 1 <= k < NQ:
                 do_QX(k - 1, 0, 4)
             if k == NQ:
@@ -329,7 +339,3 @@ def tile_tromptcell_pa_t_kernel(
                 while q_next < q_end:
                     do_QP(q_next)
                     q_next += 1
-            if k == 1:
-                for cs in halves:
-                    dst, src = regroup_views(colg, colp, cs)
-                    nc.vector.tensor_copy(out=dst, in_=src)

@@ -27,10 +27,10 @@ def tile_tromptcell_pa_t_kernel(
     with ExitStack() as ctx:
         keep = ctx.enter_context(tc.tile_pool(name="keep", bufs=1))
         prevp = ctx.enter_context(tc.tile_pool(name="prevp", bufs=6))
-        pgp = ctx.enter_context(tc.tile_pool(name="pgp", bufs=3))
+        pgp = ctx.enter_context(tc.tile_pool(name="pgp", bufs=5))
         pcp = ctx.enter_context(tc.tile_pool(name="pcp", bufs=8))
-        xgp = ctx.enter_context(tc.tile_pool(name="xgp", bufs=2))
-        xcp = ctx.enter_context(tc.tile_pool(name="xcp", bufs=5))
+        xgp = ctx.enter_context(tc.tile_pool(name="xgp", bufs=3))
+        xcp = ctx.enter_context(tc.tile_pool(name="xcp", bufs=7))
         outp = ctx.enter_context(tc.tile_pool(name="outp", bufs=10))
         psA = ctx.enter_context(tc.psum_pool(name="psA", bufs=4))
         psB = ctx.enter_context(tc.psum_pool(name="psB", bufs=4))
@@ -59,6 +59,8 @@ def tile_tromptcell_pa_t_kernel(
         nc.vector.memset(brow[:], 0.0)
         nc.vector.memset(ones_b[:], 1.0)
         nc.vector.memset(one_f[:], 1.0)
+        mhalf = keep.tile([P, 4], F32, name="mhalf")
+        nc.gpsimd.memset(mhalf[:], -0.5)
         for v, vec in enumerate((ln_prompt_w, ln_prompt_b, ln_col_w, ln_col_b)):
             nc.scalar.dma_start(out=vrows[4 * v : 4 * v + 4, :], in_=vec.rearrange("(t d) -> t d", t=4))
         nc.scalar.dma_start(out=brow[0:1, :], in_=b_imp.rearrange("(o d) -> o d", o=1))
@@ -93,7 +95,7 @@ def tile_tromptcell_pa_t_kernel(
         ident_b = keep.tile([P, P], BF16, name="ident_b")
         make_identity(nc, ident_b[:])
         warm = keep.tile([P, 1], F32, name="warm")
-        nc.scalar.activation(out=warm[:], in_=one_f[:], func=AF.Sqrt)
+        nc.scalar.activation(out=warm[:], in_=one_f[:], func=AF.Identity)
 
         pc, psc, pgt, xg, xc, xsc, osb, s1t = {}, {}, {}, {}, {}, {}, {}, {}
         wcol = {}
@@ -149,7 +151,10 @@ def tile_tromptcell_pa_t_kernel(
         def do_S2(n):
             i, b = divmod(n, 4)
             bs = slice(b * P, (b + 1) * P)
-            s2 = psA.tile([P, D], F32, name="s2_%d" % n, tag="a")
+            if i == NQ - 1:
+                s2 = psB.tile([P, D], F32, name="s2_%d" % n, tag="b")
+            else:
+                s2 = psA.tile([P, D], F32, name="s2_%d" % n, tag="a")
             nc.tensor.matmul_mx(
                 out=s2[:], lhsT=xc[i][:, bs].bitcast(FP8X4), lhsT_scale=xsc[i][:, bs],
                 rhs=wcol["colc"][:].bitcast(FP8X4), rhs_scale=wcol["cols"][:], start=True, stop=True,
@@ -157,7 +162,7 @@ def tile_tromptcell_pa_t_kernel(
             m, e = divmod(n, 2)
             if e == 0:
                 osb[m] = outp.tile([P, 2, D], F32, name="osb%d" % m, tag="osb")
-            if i == NQ - 1 and e == 1:
+            if i == NQ - 1 and b % 2 == 1:
                 nc.vector.tensor_copy(out=osb[m][:, e, :], in_=s2[:])
             else:
                 nc.scalar.copy(out=osb[m][:, e, :], in_=s2[:])
@@ -182,9 +187,9 @@ def tile_tromptcell_pa_t_kernel(
         mv0 = keep.tile([P, 2], F32, name="mv0")
         nc.vector.bn_aggr(out=mv0[:], in_=st0[:])
         ve0 = keep.tile([P, 1], F32, name="ve0")
-        nc.vector.tensor_scalar(out=ve0[:], in0=mv0[:, 1:2], scalar1=EPS, scalar2=None, op0=ALU.add)
-        sd0 = keep.tile([P, 1], F32, name="sd0")
-        nc.scalar.activation(out=sd0[:], in_=ve0[:], func=AF.Sqrt)
+        nc.gpsimd.tensor_scalar(out=ve0[:], in0=mv0[:, 1:2], scalar1=EPS, scalar2=None, op0=ALU.add)
+        rs0 = keep.tile([P, 1], F32, name="rs0")
+        nc.gpsimd.tensor_tensor(out=rs0[:], in0=ve0[:], in1=mhalf[:, 0:1], op=ALU.pow)
         c0_sb = keep.tile([P, 8, 16, 4], F32, name="c0_sb")
 
         stc = keep.tile([P, 4, 6], F32, name="stc")
@@ -196,12 +201,42 @@ def tile_tromptcell_pa_t_kernel(
         def col_aggr(i):
             nc.vector.bn_aggr(out=mvc[:, i, :], in_=stc[:, i, :])
 
+        z0 = keep.tile([P, D], F32, name="z0")
+        w1g = keep.tile([P, D, 4], BF16, name="w1g", align_bytes=64)
+        w2g = keep.tile([P, D, 4], BF16, name="w2g", align_bytes=64)
+        pnp = keep.tile([P, 4, P], BF16, name="pnp")
+        png = keep.tile([P, P, 4], BF16, name="png", align_bytes=64)
+        wcol["const"] = keep.tile([P, 8, 16, 4], F32, name="const")
+        zc = keep.tile([P, 4, D], F32, name="zc")
+        colp = keep.tile([P, 4, D], BF16, name="colp")
+        colg = keep.tile([P, D, 4], BF16, name="colg", align_bytes=64)
+        halves = (slice(0, 256), slice(256, 512))
+        ones_4 = (slice(0, 128), slice(128, 256), slice(256, 384), slice(384, 512))
+
+        def regroup(eng, g, raw, cs):
+            dst, src = regroup_views(g, raw, cs)
+            if eng == "s":
+                nc.scalar.copy(out=dst, in_=src)
+            elif eng == "v":
+                nc.vector.tensor_copy(out=dst, in_=src)
+            else:
+                nc.gpsimd.tensor_scalar(out=dst, in0=src, scalar1=1.0, scalar2=0.0, op0=ALU.mult, op1=ALU.add)
+
+        def col_T(t):
+            ct = psA.tile([P, D], F32, name="ct%d" % t, tag="a")
+            for i in range(4):
+                nc.tensor.transpose(ct[:, i * P : (i + 1) * P], zc[:, i, t * P : (t + 1) * P], ident_f[:])
+            nc.scalar.activation(
+                out=colp[:, t, :], in_=ct[:], func=AF.Identity, scale=vT[:, 8 + t : 9 + t], bias=vT[:, 12 + t : 13 + t]
+            )
+
+        def regroup_col():
+            for cs in ones_4:
+                regroup("g", colg, colp, cs)
+
         col_stats(0)
-        rs0 = keep.tile([P, 1], F32, name="rs0")
-        nc.vector.reciprocal(out=rs0[:], in_=sd0[:])
         col_stats(1)
         col_aggr(0)
-        z0 = keep.tile([P, D], F32, name="z0")
         nc.vector.tensor_scalar(
             out=z0[:], in0=p0[:], scalar1=mv0[:, 0:1], scalar2=rs0[:, 0:1], op0=ALU.subtract, op1=ALU.mult
         )
@@ -213,18 +248,22 @@ def tile_tromptcell_pa_t_kernel(
                 nc.tensor.transpose(zt[half][:, tt, :], z0[:, t * P : (t + 1) * P], ident_f[:])
         col_stats(2)
         col_aggr(1)
-
-        w1g = keep.tile([P, D, 4], BF16, name="w1g", align_bytes=64)
-        w2g = keep.tile([P, D, 4], BF16, name="w2g", align_bytes=64)
-        halves = (slice(0, 256), slice(256, 512))
-        for cs in halves:
-            dst, src = regroup_views(w1g, w1raw, cs)
-            nc.scalar.copy(out=dst, in_=src)
-        dst, src = regroup_views(w2g, w2raw, halves[0])
-        nc.vector.tensor_copy(out=dst, in_=src)
+        for c0 in range(256, 512, 64):
+            regroup("g", w1g, w1raw, slice(c0, c0 + 64))
+        regroup("s", w1g, w1raw, halves[0])
+        col_stats(3)
         col_aggr(2)
+        regroup("v", w2g, w2raw, halves[0])
+        col_aggr(3)
+        vec_ = keep.tile([P, 4], F32, name="vec_")
+        nc.gpsimd.tensor_scalar(out=vec_[:], in0=mvc[:, :, 1], scalar1=EPS, scalar2=None, op0=ALU.add)
+        rsc = keep.tile([P, 4], F32, name="rsc")
+        nc.gpsimd.tensor_tensor(out=rsc[:], in0=vec_[:], in1=mhalf[:], op=ALU.pow)
+        nmc = keep.tile([P, 4], F32, name="nmc")
+        nc.gpsimd.tensor_scalar(out=nmc[:], in0=mvc[:, :, 0], scalar1=-1.0, scalar2=None, op0=ALU.mult)
+        nmr = keep.tile([P, 4], F32, name="nmr")
+        nc.gpsimd.tensor_tensor(out=nmr[:], in0=nmc[:], in1=rsc[:], op=ALU.mult)
 
-        pnp = keep.tile([P, 4, P], BF16, name="pnp")
         for t in range(2):
             nc.scalar.activation(
                 out=pnp[:, t, :], in_=zt[0][:, t, :], func=AF.Identity, scale=vT[:, t : t + 1], bias=vT[:, 4 + t : 5 + t]
@@ -235,18 +274,21 @@ def tile_tromptcell_pa_t_kernel(
                 out=pnp[:, t, :], in0=zt[1][:, t - 2, :], scalar1=vT[:, t : t + 1], scalar2=vT[:, 4 + t : 5 + t],
                 op0=ALU.mult, op1=ALU.add,
             )
-        dst, src = regroup_views(w2g, w2raw, halves[1])
-        nc.vector.tensor_copy(out=dst, in_=src)
-        png = keep.tile([P, P, 4], BF16, name="png", align_bytes=64)
+        regroup("s", w2g, w2raw, halves[1])
         nc.vector.tensor_copy(out=png[:], in_=pnp[:].rearrange("p t q -> p q t"))
         w1c, w1s = quantise("w1", w1g, D)
         pnc, pns = quantise("pn", png, P)
-        col_stats(3)
-        wcol["w2c"], wcol["w2s"] = quantise("w2", w2g, D)
-
+        for i in range(4):
+            nc.vector.tensor_scalar(
+                out=zc[:, i, :], in0=colraw[:, i, :], scalar1=mvc[:, i, 0:1], scalar2=rsc[:, i : i + 1],
+                op0=ALU.subtract, op1=ALU.mult,
+            )
         do_T(0)
         do_T(1)
         load_prev(6, 1)
+        do_QP(0)
+        wcol["w2c"], wcol["w2s"] = quantise("w2", w2g, D)
+
         fp_ps = psB.tile([P, 4, P], F32, name="fp_ps", tag="b")
         for t in range(4):
             ts = slice(t * P, (t + 1) * P)
@@ -254,80 +296,48 @@ def tile_tromptcell_pa_t_kernel(
                 out=fp_ps[:, t, :], lhsT=w1c[:, ts].bitcast(FP8X4), lhsT_scale=w1s[:, ts],
                 rhs=pnc[:].bitcast(FP8X4), rhs_scale=pns[:], start=True, stop=True,
             )
-        wcol["const"] = keep.tile([P, 8, 16, 4], F32, name="const")
         nc.vector.tensor_tensor(
             out=wcol["const"][:], in0=fp_ps[:].rearrange("p t (b j) -> p j b t", j=8), in1=c0_sb[:], op=ALU.add
         )
-        col_aggr(3)
-        vec_ = keep.tile([P, 4], F32, name="vec_")
-        nc.vector.tensor_scalar(out=vec_[:], in0=mvc[:, :, 1], scalar1=EPS, scalar2=None, op0=ALU.add)
-        nmc = keep.tile([P, 4], F32, name="nmc")
-        nc.vector.tensor_scalar(out=nmc[:], in0=mvc[:, :, 0], scalar1=-1.0, scalar2=None, op0=ALU.mult)
-        do_QP(0)
+        for t in range(4):
+            col_T(t)
+        for n in range(4):
+            do_S1(n)
         do_T(2)
-        sdc = keep.tile([P, 4], F32, name="sdc")
-        nc.scalar.activation(out=sdc[:], in_=vec_[:], func=AF.Sqrt)
         do_QP(1)
-        rsc = keep.tile([P, 4], F32, name="rsc")
-        nc.vector.reciprocal(out=rsc[:], in_=sdc[:])
+        regroup_col()
         do_T(3)
         load_prev(7, 1)
-        zc = keep.tile([P, 4, D], F32, name="zc")
-        do_QP(2)
-        nmr = keep.tile([P, 4], F32, name="nmr")
-        nc.vector.tensor_tensor(out=nmr[:], in0=nmc[:], in1=rsc[:], op=ALU.mult)
-        for i in range(4):
-            nc.scalar.activation(
-                out=zc[:, i, :], in_=colraw[:, i, :], func=AF.Identity, scale=rsc[:, i : i + 1], bias=nmr[:, i : i + 1]
-            )
-        for n in range(3):
-            do_S1(n)
 
-        colp = keep.tile([P, 4, D], BF16, name="colp")
-        colg = keep.tile([P, D, 4], BF16, name="colg", align_bytes=64)
-
-        def col_transposed():
-            for t in range(4):
-                ct = psA.tile([P, D], F32, name="ct%d" % t, tag="a")
-                for i in range(4):
-                    nc.tensor.transpose(ct[:, i * P : (i + 1) * P], zc[:, i, t * P : (t + 1) * P], ident_f[:])
-                nc.scalar.activation(
-                    out=colp[:, t, :], in_=ct[:], func=AF.Identity, scale=vT[:, 8 + t : 9 + t], bias=vT[:, 12 + t : 13 + t]
-                )
-
-        t_next, q_next, s2_next = 4, 3, 0
+        t_next, q_next, s2_next = 4, 2, 0
         for k in range(NQ + 1):
             last = k == NQ - 1
             if k < NQ:
                 do_XE(4 * k)
-            if k == 2:
-                for cs in halves:
-                    dst, src = regroup_views(colg, colp, cs)
-                    nc.vector.tensor_copy(out=dst, in_=src)
             if 1 <= k < NQ:
                 do_QX(k - 1, 0, 4)
             if k == NQ:
                 do_QX(k - 1, 2, 3)
                 do_QX(k - 1, 3, 4)
-            if k == 2:
+            if k == 1:
                 wcol["colc"], wcol["cols"] = quantise("col", colg, D)
             n_s2 = 0
-            if k >= 2:
+            if k >= 1:
                 n_s2 = min(4 * k - s2_next, 4 if t_next < NQ else 6)
                 if k == NQ:
                     n_s2 = NB - s2_next
-            q_end = t_next
+            while q_next < min(t_next, k + 2):
+                do_QP(q_next)
+                q_next += 1
             for b in range(4):
-                if 4 * k + 3 + b < NB:
-                    do_S1(4 * k + 3 + b)
-                if k == 1 and b == 0:
-                    col_transposed()
+                if 4 * k + 4 + b < NB:
+                    do_S1(4 * k + 4 + b)
                 c = -(-n_s2 // (4 - b))
                 n_s2 -= c
                 for r in range(c):
                     do_S2(s2_next)
                     s2_next += 1
-            for r in range(2 if k == 1 else 1):
+            for r in range(2 if False else 1):
                 if t_next < NQ:
                     do_T(t_next)
                     t_next += 1
@@ -336,6 +346,3 @@ def tile_tromptcell_pa_t_kernel(
                     do_XE(4 * k + b)
                     if last and b == 2:
                         do_QX(k, 0, 2)
-                while q_next < q_end:
-                    do_QP(q_next)
-                    q_next += 1

@@ -59,8 +59,6 @@ def tile_tromptcell_pa_t_kernel(
         nc.vector.memset(brow[:], 0.0)
         nc.vector.memset(ones_b[:], 1.0)
         nc.vector.memset(one_f[:], 1.0)
-        mhalf = keep.tile([P, 4], F32, name="mhalf")
-        nc.gpsimd.memset(mhalf[:], -0.5)
         for v, vec in enumerate((ln_prompt_w, ln_prompt_b, ln_col_w, ln_col_b)):
             nc.scalar.dma_start(out=vrows[4 * v : 4 * v + 4, :], in_=vec.rearrange("(t d) -> t d", t=4))
         nc.scalar.dma_start(out=brow[0:1, :], in_=b_imp.rearrange("(o d) -> o d", o=1))
@@ -68,7 +66,7 @@ def tile_tromptcell_pa_t_kernel(
         p0 = keep.tile([P, D], BF16, name="p0")
         nc.sync.dma_start(out=p0[:], in_=emb_prompt)
         colraw = keep.tile([P, 4, D], BF16, name="colraw")
-        nc.sync.dma_start(out=colraw[:], in_=emb_column.rearrange("(i p) d -> p i d", p=P))
+        nc.sync.dma_start(out=colraw[:], in_=emb_column.rearrange("(p i) d -> p i d", i=4))
         w1raw = keep.tile([P, 4, D], BF16, name="w1raw")
         nc.sync.dma_start(out=w1raw[:], in_=W_imp[0:D, :].rearrange("(t p) c -> p t c", p=P))
         w2raw = keep.tile([P, 4, D], BF16, name="w2raw")
@@ -95,7 +93,7 @@ def tile_tromptcell_pa_t_kernel(
         ident_b = keep.tile([P, P], BF16, name="ident_b")
         make_identity(nc, ident_b[:])
         warm = keep.tile([P, 1], F32, name="warm")
-        nc.scalar.activation(out=warm[:], in_=one_f[:], func=AF.Identity)
+        nc.scalar.activation(out=warm[:], in_=one_f[:], func=AF.Abs_reciprocal_sqrt)
 
         pc, psc, pgt, xg, xc, xsc, osb, s1t = {}, {}, {}, {}, {}, {}, {}, {}
         wcol = {}
@@ -186,10 +184,8 @@ def tile_tromptcell_pa_t_kernel(
         nc.vector.bn_stats(out=st0[:], in_=p0[:])
         mv0 = keep.tile([P, 2], F32, name="mv0")
         nc.vector.bn_aggr(out=mv0[:], in_=st0[:])
-        ve0 = keep.tile([P, 1], F32, name="ve0")
-        nc.gpsimd.tensor_scalar(out=ve0[:], in0=mv0[:, 1:2], scalar1=EPS, scalar2=None, op0=ALU.add)
         rs0 = keep.tile([P, 1], F32, name="rs0")
-        nc.gpsimd.tensor_tensor(out=rs0[:], in0=ve0[:], in1=mhalf[:, 0:1], op=ALU.pow)
+        nc.scalar.activation(out=rs0[:], in_=mv0[:, 1:2], func=AF.Abs_reciprocal_sqrt, bias=EPS)
         c0_sb = keep.tile([P, 8, 16, 4], F32, name="c0_sb")
 
         stc = keep.tile([P, 4, 6], F32, name="stc")
@@ -227,7 +223,8 @@ def tile_tromptcell_pa_t_kernel(
             for i in range(4):
                 nc.tensor.transpose(ct[:, i * P : (i + 1) * P], zc[:, i, t * P : (t + 1) * P], ident_f[:])
             nc.scalar.activation(
-                out=colp[:, t, :], in_=ct[:], func=AF.Identity, scale=vT[:, 8 + t : 9 + t], bias=vT[:, 12 + t : 13 + t]
+                out=colp[:, t, :].rearrange("p (c i) -> p c i", i=4), in_=ct[:].rearrange("p (i c) -> p c i", i=4),
+                func=AF.Identity, scale=vT[:, 8 + t : 9 + t], bias=vT[:, 12 + t : 13 + t]
             )
 
         def regroup_col():
@@ -248,21 +245,12 @@ def tile_tromptcell_pa_t_kernel(
                 nc.tensor.transpose(zt[half][:, tt, :], z0[:, t * P : (t + 1) * P], ident_f[:])
         col_stats(2)
         col_aggr(1)
-        for c0 in range(256, 512, 64):
-            regroup("g", w1g, w1raw, slice(c0, c0 + 64))
-        regroup("s", w1g, w1raw, halves[0])
+        for cs in halves:
+            regroup("s", w1g, w1raw, cs)
         col_stats(3)
         col_aggr(2)
         regroup("v", w2g, w2raw, halves[0])
         col_aggr(3)
-        vec_ = keep.tile([P, 4], F32, name="vec_")
-        nc.gpsimd.tensor_scalar(out=vec_[:], in0=mvc[:, :, 1], scalar1=EPS, scalar2=None, op0=ALU.add)
-        rsc = keep.tile([P, 4], F32, name="rsc")
-        nc.gpsimd.tensor_tensor(out=rsc[:], in0=vec_[:], in1=mhalf[:], op=ALU.pow)
-        nmc = keep.tile([P, 4], F32, name="nmc")
-        nc.gpsimd.tensor_scalar(out=nmc[:], in0=mvc[:, :, 0], scalar1=-1.0, scalar2=None, op0=ALU.mult)
-        nmr = keep.tile([P, 4], F32, name="nmr")
-        nc.gpsimd.tensor_tensor(out=nmr[:], in0=nmc[:], in1=rsc[:], op=ALU.mult)
 
         for t in range(2):
             nc.scalar.activation(
@@ -274,7 +262,9 @@ def tile_tromptcell_pa_t_kernel(
                 out=pnp[:, t, :], in0=zt[1][:, t - 2, :], scalar1=vT[:, t : t + 1], scalar2=vT[:, 4 + t : 5 + t],
                 op0=ALU.mult, op1=ALU.add,
             )
-        regroup("s", w2g, w2raw, halves[1])
+        rsc = keep.tile([P, 4], F32, name="rsc")
+        nc.scalar.activation(out=rsc[:], in_=mvc[:, :, 1], func=AF.Abs_reciprocal_sqrt, bias=EPS)
+        regroup("v", w2g, w2raw, halves[1])
         nc.vector.tensor_copy(out=png[:], in_=pnp[:].rearrange("p t q -> p q t"))
         w1c, w1s = quantise("w1", w1g, D)
         pnc, pns = quantise("pn", png, P)

@@ -31,6 +31,7 @@ def tile_tromptcell_pa_t_kernel(
         pcp = ctx.enter_context(tc.tile_pool(name="pcp", bufs=8))
         xgp = ctx.enter_context(tc.tile_pool(name="xgp", bufs=3))
         xcp = ctx.enter_context(tc.tile_pool(name="xcp", bufs=7))
+        s1cp = ctx.enter_context(tc.tile_pool(name="s1cp", bufs=2))
         outp = ctx.enter_context(tc.tile_pool(name="outp", bufs=10))
         psA = ctx.enter_context(tc.psum_pool(name="psA", bufs=4))
         psB = ctx.enter_context(tc.psum_pool(name="psB", bufs=4))
@@ -59,9 +60,6 @@ def tile_tromptcell_pa_t_kernel(
         nc.vector.memset(brow[:], 0.0)
         nc.vector.memset(ones_b[:], 1.0)
         nc.vector.memset(one_f[:], 1.0)
-        for v, vec in enumerate((ln_prompt_w, ln_prompt_b, ln_col_w, ln_col_b)):
-            nc.scalar.dma_start(out=vrows[4 * v : 4 * v + 4, :], in_=vec.rearrange("(t d) -> t d", t=4))
-        nc.scalar.dma_start(out=brow[0:1, :], in_=b_imp.rearrange("(o d) -> o d", o=1))
 
         p0 = keep.tile([P, D], BF16, name="p0")
         nc.sync.dma_start(out=p0[:], in_=emb_prompt)
@@ -74,6 +72,9 @@ def tile_tromptcell_pa_t_kernel(
             out=w2raw[:].rearrange("p (u e) c -> p u (e c)", u=2),
             in_=W_imp[D : 2 * D, :].rearrange("(u w e) c -> w u (e c)", u=2, e=2),
         )
+        for v, vec in enumerate((ln_prompt_w, ln_prompt_b, ln_col_w, ln_col_b)):
+            nc.scalar.dma_start(out=vrows[4 * v : 4 * v + 4, :], in_=vec.rearrange("(t d) -> t d", t=4))
+        nc.scalar.dma_start(out=brow[0:1, :], in_=b_imp.rearrange("(o d) -> o d", o=1))
         prev_sb = {}
 
         def load_prev(g, pieces):
@@ -95,7 +96,7 @@ def tile_tromptcell_pa_t_kernel(
         warm = keep.tile([P, 1], F32, name="warm")
         nc.scalar.activation(out=warm[:], in_=one_f[:], func=AF.Abs_reciprocal_sqrt)
 
-        pc, psc, pgt, xg, xc, xsc, osb, s1t = {}, {}, {}, {}, {}, {}, {}, {}
+        pc, psc, pgt, xg, xc, xsc, osb, s1t, s1c = {}, {}, {}, {}, {}, {}, {}, {}, {}
         wcol = {}
 
         def do_T(i):
@@ -128,10 +129,23 @@ def tile_tromptcell_pa_t_kernel(
                     rhs=pc[i][:, bs].bitcast(FP8X4), rhs_scale=psc[i][:, bs], start=True, stop=True,
                 )
 
+            if b == 2 and i in (7, 12):
+                s1c[n] = s1cp.tile([P, P, 4], F32, name="s1c%d" % n, tag="s1c")
+                nc.scalar.copy(out=s1c[n][:], in_=s1t[n][:].rearrange("p t q -> p q t"))
+
         def do_XE(n):
             i, b = divmod(n, 4)
             if b == 0:
                 xg[i] = xgp.tile([P, 4 * D], BF16, name="xg%d" % i, tag="xg", align_bytes=64)
+            if b == 2 and i in (7, 12):
+                for a0 in range(0, 8, 4):
+                    nc.gpsimd.tensor_tensor(
+                        out=xg[i][:, b * D : (b + 1) * D].rearrange("p (a b t) -> p a b t", a=8, t=4)[:, a0 : a0 + 4],
+                        in0=s1c[n][:].rearrange("p (a b) t -> p a b t", a=8)[:, a0 : a0 + 4],
+                        in1=wcol["const"][:, n % 8].unsqueeze(1).to_broadcast([P, 4, 16, 4]),
+                        op=ALU.add,
+                    )
+                return
             nc.vector.tensor_tensor(
                 out=xg[i][:, b * D : (b + 1) * D].rearrange("p (a b t) -> p a b t", a=8, t=4),
                 in0=s1t[n][:].rearrange("p t (a b) -> p a b t", a=8),
@@ -160,7 +174,7 @@ def tile_tromptcell_pa_t_kernel(
             m, e = divmod(n, 2)
             if e == 0:
                 osb[m] = outp.tile([P, 2, D], F32, name="osb%d" % m, tag="osb")
-            if i == NQ - 1 and b % 2 == 1:
+            if i == NQ - 1 and b >= 2:
                 nc.vector.tensor_copy(out=osb[m][:, e, :], in_=s2[:])
             else:
                 nc.scalar.copy(out=osb[m][:, e, :], in_=s2[:])
@@ -305,7 +319,7 @@ def tile_tromptcell_pa_t_kernel(
             if k < NQ:
                 do_XE(4 * k)
             if 1 <= k < NQ:
-                do_QX(k - 1, 0, 4)
+                do_QX(k - 1, 2 if k - 1 >= 13 else 0, 4)
             if k == NQ:
                 do_QX(k - 1, 2, 3)
                 do_QX(k - 1, 3, 4)
@@ -334,5 +348,9 @@ def tile_tromptcell_pa_t_kernel(
             if k < NQ:
                 for b in range(1, 4):
                     do_XE(4 * k + b)
-                    if last and b == 2:
+                    if k >= 13 and b == 2:
                         do_QX(k, 0, 2)
+                if k >= 13:
+                    for r in range(2):
+                        do_S2(s2_next)
+                        s2_next += 1

from contextlib import ExitStack

import concourse.mybir as mybir
from concourse.masks import make_identity

F32 = mybir.dt.float32
BF16 = mybir.dt.bfloat16
U32 = mybir.dt.uint32
U8 = mybir.dt.uint8
FP8X4 = mybir.dt.float8_e4m3fn_x4
AF = mybir.ActivationFunctionType
ALU = mybir.AluOpType

P = 128
D = 512
NB = 64
NQ = 16
NG = 8
EPS = 1e-5
FLOPS = 2 * 64 * 128 * 512 * 512 * 2 + 2 * 128 * 512 * 512


def tile_tromptcell_pa_t_kernel(
    tc, prev_cell_out, emb_prompt, ln_prompt_w, ln_prompt_b, W_imp, b_imp, emb_column, ln_col_w, ln_col_b, out
):
    nc = tc.nc
    with ExitStack() as ctx:
        keep = ctx.enter_context(tc.tile_pool(name="keep", bufs=1))
        prevp = ctx.enter_context(tc.tile_pool(name="prevp", bufs=6))
        pgp = ctx.enter_context(tc.tile_pool(name="pgp", bufs=5))
        pcp = ctx.enter_context(tc.tile_pool(name="pcp", bufs=8))
        xgp = ctx.enter_context(tc.tile_pool(name="xgp", bufs=3))
        xcp = ctx.enter_context(tc.tile_pool(name="xcp", bufs=7))
        s1cp = ctx.enter_context(tc.tile_pool(name="s1cp", bufs=2))
        outp = ctx.enter_context(tc.tile_pool(name="outp", bufs=10))
        psA = ctx.enter_context(tc.psum_pool(name="psA", bufs=4))
        psB = ctx.enter_context(tc.psum_pool(name="psB", bufs=4))
        ctx.enter_context(tc.manual_schedule())

        prev_v = prev_cell_out.flatten_outer_dims().rearrange("(g q j) d -> g q (j d)", q=P, j=8)
        out_v = out.flatten_outer_dims().rearrange("(g q j) c -> g q j c", q=P, j=8)

        def regroup_views(dst, src, cs):
            return (
                dst[:, cs, :].rearrange("p (c i) t -> p c t i", i=4),
                src[:, :, cs].rearrange("p t (c i) -> p c t i", i=4),
            )

        def quantise(name, grouped, width):
            codes = keep.tile([P, width], U32, name=name + "c", align_bytes=64)
            scales = keep.tile([P, width], U8, name=name + "s", align_bytes=64)
            nc.vector.quantize_mx(out=codes[:].bitcast(FP8X4), scales=scales[:], in_=grouped[:].rearrange("p c t -> p (c t)"))
            return codes, scales

        vrows = keep.tile([P, P], BF16, name="vrows")
        brow = keep.tile([P, D], BF16, name="brow")
        ones_b = keep.tile([P, P], BF16, name="ones_b")
        one_f = keep.tile([P, 1], F32, name="one_f")
        nc.vector.memset(vrows[:], 0.0)
        nc.vector.memset(brow[:], 0.0)
        nc.vector.memset(ones_b[:], 1.0)
        nc.vector.memset(one_f[:], 1.0)

        p0 = keep.tile([P, D], BF16, name="p0")
        nc.sync.dma_start(out=p0[:], in_=emb_prompt)
        colraw = keep.tile([P, 4, D], BF16, name="colraw")
        nc.sync.dma_start(out=colraw[:], in_=emb_column.rearrange("(p i) d -> p i d", i=4))
        w1raw = keep.tile([P, 4, D], BF16, name="w1raw")
        nc.sync.dma_start(out=w1raw[:], in_=W_imp[0:D, :].rearrange("(t p) c -> p t c", p=P))
        w2raw = keep.tile([P, 4, D], BF16, name="w2raw")
        nc.sync.dma_start(
            out=w2raw[:].rearrange("p (u e) c -> p u (e c)", u=2),
            in_=W_imp[D : 2 * D, :].rearrange("(u w e) c -> w u (e c)", u=2, e=2),
        )
        for v, vec in enumerate((ln_prompt_w, ln_prompt_b, ln_col_w, ln_col_b)):
            nc.scalar.dma_start(out=vrows[4 * v : 4 * v + 4, :], in_=vec.rearrange("(t d) -> t d", t=4))
        nc.scalar.dma_start(out=brow[0:1, :], in_=b_imp.rearrange("(o d) -> o d", o=1))
        prev_sb = {}

        def load_prev(g, pieces):
            t = prevp.tile([P, 8 * D], BF16, name="prev%d" % g, tag="prev")
            prev_sb[g] = t
            w = 8 * D // pieces
            for s in range(pieces):
                nc.sync.dma_start(out=t[:, s * w : (s + 1) * w], in_=prev_v[g][:, s * w : (s + 1) * w])

        load_prev(0, 2)
        load_prev(1, 2)
        for g in range(2, 6):
            load_prev(g, 1)

        ident_f = keep.tile([P, P], F32, name="ident_f")
        make_identity(nc, ident_f[:])
        ident_b = keep.tile([P, P], BF16, name="ident_b")
        make_identity(nc, ident_b[:])
        warm = keep.tile([P, 1], F32, name="warm")
        nc.scalar.activation(out=warm[:], in_=one_f[:], func=AF.Abs_reciprocal_sqrt)

        pc, psc, pgt, xg, xc, xsc, osb, s1t, s1c = {}, {}, {}, {}, {}, {}, {}, {}, {}
        wcol = {}

        def do_T(i):
            g, h = divmod(i, 2)
            src = prev_sb[g][:].bitcast(F32)
            pgt[i] = pgp.tile([P, 4 * D], BF16, name="pg%d" % i, tag="pg", align_bytes=64)
            pg32 = pgt[i][:].bitcast(F32).rearrange("p (b q u) -> p b q u", b=4, u=2)
            for half in range(2):
                tp = psA.tile([P, 2, 2, P], F32, name="tp%d_%d" % (i, half), tag="a")
                for bb in range(2):
                    j = 4 * h + 2 * half + bb
                    for u in range(2):
                        o = 256 * j + P * u
                        nc.tensor.transpose(tp[:, bb, u, :], src[:, o : o + P], ident_f[:])
                nc.scalar.copy(out=pg32[:, 2 * half : 2 * half + 2], in_=tp[:].rearrange("p b u q -> p b q u"))

        def do_QP(i):
            pc[i] = pcp.tile([P, D], U32, name="pc%d" % i, tag="pc", align_bytes=64)
            psc[i] = pcp.tile([P, D], U8, name="psc%d" % i, tag="psc", align_bytes=64)
            nc.vector.quantize_mx(out=pc[i][:].bitcast(FP8X4), scales=psc[i][:], in_=pgt[i][:])

        def do_S1(n):
            i, b = divmod(n, 4)
            bs = slice(b * P, (b + 1) * P)
            s1t[n] = psB.tile([P, 4, P], F32, name="s1_%d" % n, tag="b")
            for t in range(4):
                ts = slice(t * P, (t + 1) * P)
                nc.tensor.matmul_mx(
                    out=s1t[n][:, t, :], lhsT=wcol["w2c"][:, ts].bitcast(FP8X4), lhsT_scale=wcol["w2s"][:, ts],
                    rhs=pc[i][:, bs].bitcast(FP8X4), rhs_scale=psc[i][:, bs], start=True, stop=True,
                )

            if b == 2 and i in (7, 12):
                s1c[n] = s1cp.tile([P, P, 4], F32, name="s1c%d" % n, tag="s1c")
                nc.scalar.copy(out=s1c[n][:], in_=s1t[n][:].rearrange("p t q -> p q t"))

        def do_XE(n):
            i, b = divmod(n, 4)
            if b == 0:
                xg[i] = xgp.tile([P, 4 * D], BF16, name="xg%d" % i, tag="xg", align_bytes=64)
            if b == 2 and i in (7, 12):
                for a0 in range(0, 8, 4):
                    nc.gpsimd.tensor_tensor(
                        out=xg[i][:, b * D : (b + 1) * D].rearrange("p (a b t) -> p a b t", a=8, t=4)[:, a0 : a0 + 4],
                        in0=s1c[n][:].rearrange("p (a b) t -> p a b t", a=8)[:, a0 : a0 + 4],
                        in1=wcol["const"][:, n % 8].unsqueeze(1).to_broadcast([P, 4, 16, 4]),
                        op=ALU.add,
                    )
                return
            nc.vector.tensor_tensor(
                out=xg[i][:, b * D : (b + 1) * D].rearrange("p (a b t) -> p a b t", a=8, t=4),
                in0=s1t[n][:].rearrange("p t (a b) -> p a b t", a=8),
                in1=wcol["const"][:, n % 8].unsqueeze(1).to_broadcast([P, 8, 16, 4]),
                op=ALU.add,
            )

        def do_QX(i, b0, b1):
            if b0 == 0:
                xc[i] = xcp.tile([P, D], U32, name="xc%d" % i, tag="xc", align_bytes=64)
                xsc[i] = xcp.tile([P, D], U8, name="xsc%d" % i, tag="xsc", align_bytes=64)
            cs = slice(b0 * P, b1 * P)
            nc.vector.quantize_mx(out=xc[i][:, cs].bitcast(FP8X4), scales=xsc[i][:, cs], in_=xg[i][:, b0 * D : b1 * D])

        def do_S2(n):
            i, b = divmod(n, 4)
            bs = slice(b * P, (b + 1) * P)
            if i == NQ - 1:
                s2 = psB.tile([P, D], F32, name="s2_%d" % n, tag="b")
            else:
                s2 = psA.tile([P, D], F32, name="s2_%d" % n, tag="a")
            nc.tensor.matmul_mx(
                out=s2[:], lhsT=xc[i][:, bs].bitcast(FP8X4), lhsT_scale=xsc[i][:, bs],
                rhs=wcol["colc"][:].bitcast(FP8X4), rhs_scale=wcol["cols"][:], start=True, stop=True,
            )
            m, e = divmod(n, 2)
            if e == 0:
                osb[m] = outp.tile([P, 2, D], F32, name="osb%d" % m, tag="osb")
            if i == NQ - 1 and b >= 2:
                nc.vector.tensor_copy(out=osb[m][:, e, :], in_=s2[:])
            else:
                nc.scalar.copy(out=osb[m][:, e, :], in_=s2[:])
            g, j = divmod(n, 8)
            if n >= NB - 2:
                nc.sync.dma_start(out=out_v[g][:, j, :], in_=osb[m][:, e, :])
            elif e == 1:
                nc.sync.dma_start(out=out_v[g][:, j - 1 : j + 1, :], in_=osb[m][:])

        vt_ps = psA.tile([P, P], BF16, name="vt_ps", tag="a")
        nc.tensor.transpose(vt_ps[:], vrows[:], ident_b[:])
        vT = keep.tile([P, 16], F32, name="vT")
        nc.scalar.copy(out=vT[:], in_=vt_ps[:, 0:16])

        c0_ps = psA.tile([P, 4, P], F32, name="c0_ps", tag="a")
        for t in range(4):
            nc.tensor.matmul(out=c0_ps[:, t, :], lhsT=p0[:, t * P : (t + 1) * P], rhs=ident_b[:], start=True, stop=False)
            nc.tensor.matmul(out=c0_ps[:, t, :], lhsT=brow[:, t * P : (t + 1) * P], rhs=ones_b[:], start=False, stop=True)

        st0 = keep.tile([P, 6], F32, name="st0")
        nc.vector.bn_stats(out=st0[:], in_=p0[:])
        mv0 = keep.tile([P, 2], F32, name="mv0")
        nc.vector.bn_aggr(out=mv0[:], in_=st0[:])
        rs0 = keep.tile([P, 1], F32, name="rs0")
        nc.scalar.activation(out=rs0[:], in_=mv0[:, 1:2], func=AF.Abs_reciprocal_sqrt, bias=EPS)
        c0_sb = keep.tile([P, 8, 16, 4], F32, name="c0_sb")

        stc = keep.tile([P, 4, 6], F32, name="stc")
        mvc = keep.tile([P, 4, 2], F32, name="mvc")

        def col_stats(i):
            nc.vector.bn_stats(out=stc[:, i, :], in_=colraw[:, i, :])

        def col_aggr(i):
            nc.vector.bn_aggr(out=mvc[:, i, :], in_=stc[:, i, :])

        z0 = keep.tile([P, D], F32, name="z0")
        w1g = keep.tile([P, D, 4], BF16, name="w1g", align_bytes=64)
        w2g = keep.tile([P, D, 4], BF16, name="w2g", align_bytes=64)
        pnp = keep.tile([P, 4, P], BF16, name="pnp")
        png = keep.tile([P, P, 4], BF16, name="png", align_bytes=64)
        wcol["const"] = keep.tile([P, 8, 16, 4], F32, name="const")
        zc = keep.tile([P, 4, D], F32, name="zc")
        colp = keep.tile([P, 4, D], BF16, name="colp")
        colg = keep.tile([P, D, 4], BF16, name="colg", align_bytes=64)
        halves = (slice(0, 256), slice(256, 512))
        ones_4 = (slice(0, 128), slice(128, 256), slice(256, 384), slice(384, 512))

        def regroup(eng, g, raw, cs):
            dst, src = regroup_views(g, raw, cs)
            if eng == "s":
                nc.scalar.copy(out=dst, in_=src)
            elif eng == "v":
                nc.vector.tensor_copy(out=dst, in_=src)
            else:
                nc.gpsimd.tensor_scalar(out=dst, in0=src, scalar1=1.0, scalar2=0.0, op0=ALU.mult, op1=ALU.add)

        def col_T(t):
            ct = psA.tile([P, D], F32, name="ct%d" % t, tag="a")
            for i in range(4):
                nc.tensor.transpose(ct[:, i * P : (i + 1) * P], zc[:, i, t * P : (t + 1) * P], ident_f[:])
            nc.scalar.activation(
                out=colp[:, t, :].rearrange("p (c i) -> p c i", i=4), in_=ct[:].rearrange("p (i c) -> p c i", i=4),
                func=AF.Identity, scale=vT[:, 8 + t : 9 + t], bias=vT[:, 12 + t : 13 + t]
            )

        def regroup_col():
            for cs in ones_4:
                regroup("g", colg, colp, cs)

        col_stats(0)
        col_stats(1)
        col_aggr(0)
        nc.vector.tensor_scalar(
            out=z0[:], in0=p0[:], scalar1=mv0[:, 0:1], scalar2=rs0[:, 0:1], op0=ALU.subtract, op1=ALU.mult
        )
        zt = []
        for half in range(2):
            zt.append(psB.tile([P, 2, P], F32, name="zt%d" % half, tag="b"))
            for tt in range(2):
                t = 2 * half + tt
                nc.tensor.transpose(zt[half][:, tt, :], z0[:, t * P : (t + 1) * P], ident_f[:])
        col_stats(2)
        col_aggr(1)
        for cs in halves:
            regroup("s", w1g, w1raw, cs)
        col_stats(3)
        col_aggr(2)
        regroup("v", w2g, w2raw, halves[0])
        col_aggr(3)

        for t in range(2):
            nc.scalar.activation(
                out=pnp[:, t, :], in_=zt[0][:, t, :], func=AF.Identity, scale=vT[:, t : t + 1], bias=vT[:, 4 + t : 5 + t]
            )
        nc.scalar.copy(out=c0_sb[:], in_=c0_ps[:].rearrange("p t (b j) -> p j b t", j=8))
        for t in range(2, 4):
            nc.vector.tensor_scalar(
                out=pnp[:, t, :], in0=zt[1][:, t - 2, :], scalar1=vT[:, t : t + 1], scalar2=vT[:, 4 + t : 5 + t],
                op0=ALU.mult, op1=ALU.add,
            )
        rsc = keep.tile([P, 4], F32, name="rsc")
        nc.scalar.activation(out=rsc[:], in_=mvc[:, :, 1], func=AF.Abs_reciprocal_sqrt, bias=EPS)
        regroup("v", w2g, w2raw, halves[1])
        nc.vector.tensor_copy(out=png[:], in_=pnp[:].rearrange("p t q -> p q t"))
        w1c, w1s = quantise("w1", w1g, D)
        pnc, pns = quantise("pn", png, P)
        for i in range(4):
            nc.vector.tensor_scalar(
                out=zc[:, i, :], in0=colraw[:, i, :], scalar1=mvc[:, i, 0:1], scalar2=rsc[:, i : i + 1],
                op0=ALU.subtract, op1=ALU.mult,
            )
        do_T(0)
        do_T(1)
        load_prev(6, 1)
        do_QP(0)
        wcol["w2c"], wcol["w2s"] = quantise("w2", w2g, D)

        fp_ps = psB.tile([P, 4, P], F32, name="fp_ps", tag="b")
        for t in range(4):
            ts = slice(t * P, (t + 1) * P)
            nc.tensor.matmul_mx(
                out=fp_ps[:, t, :], lhsT=w1c[:, ts].bitcast(FP8X4), lhsT_scale=w1s[:, ts],
                rhs=pnc[:].bitcast(FP8X4), rhs_scale=pns[:], start=True, stop=True,
            )
        nc.vector.tensor_tensor(
            out=wcol["const"][:], in0=fp_ps[:].rearrange("p t (b j) -> p j b t", j=8), in1=c0_sb[:], op=ALU.add
        )
        for t in range(4):
            col_T(t)
        for n in range(4):
            do_S1(n)
        do_T(2)
        do_QP(1)
        regroup_col()
        do_T(3)
        load_prev(7, 1)

        t_next, q_next, s2_next = 4, 2, 0
        for k in range(NQ + 1):
            last = k == NQ - 1
            if k < NQ:
                do_XE(4 * k)
            if 1 <= k < NQ:
                do_QX(k - 1, 2 if k - 1 >= 13 else 0, 4)
            if k == NQ:
                do_QX(k - 1, 2, 3)
                do_QX(k - 1, 3, 4)
            if k == 1:
                wcol["colc"], wcol["cols"] = quantise("col", colg, D)
            n_s2 = 0
            if k >= 1:
                n_s2 = min(4 * k - s2_next, 4 if t_next < NQ else 6)
                if k == NQ:
                    n_s2 = NB - s2_next
            while q_next < min(t_next, k + 2):
                do_QP(q_next)
                q_next += 1
            for b in range(4):
                if 4 * k + 4 + b < NB:
                    do_S1(4 * k + 4 + b)
                c = -(-n_s2 // (4 - b))
                n_s2 -= c
                for r in range(c):
                    do_S2(s2_next)
                    s2_next += 1
            for r in range(2 if False else 1):
                if t_next < NQ:
                    do_T(t_next)
                    t_next += 1
            if k < NQ:
                for b in range(1, 4):
                    do_XE(4 * k + b)
                    if k >= 13 and b == 2:
                        do_QX(k, 0, 2)
                if k >= 13:
                    for r in range(2):
                        do_S2(s2_next)
                        s2_next += 1
